import numpy as np
import ml_dtypes


def mxq(x, axis, fmt="e4m3"):
    dtype, down = {"e4m3": (ml_dtypes.float8_e4m3fn, 7), "e5m2": (ml_dtypes.float8_e5m2, 14)}[fmt]
    v = np.moveaxis(np.asarray(x, np.float32).astype(ml_dtypes.bfloat16).astype(np.float64), axis, -1)
    blocks = v.reshape(v.shape[:-1] + (-1, 32))
    amax = np.abs(blocks).max(-1, keepdims=True)
    byte = np.maximum(np.where(amax > 0, np.frexp(amax)[1] - 1 + 127, 0) - down, 1)
    scale = np.exp2(byte - 127.0)
    codes = (blocks / scale).astype(np.float32).astype(dtype).astype(np.float64)
    return np.moveaxis((codes * scale).reshape(v.shape), -1, axis)


WIDE = False


def mx_kscale(k):
    if not WIDE:
        return np.ones(k)
    levels = np.array([10, -10, 5, -5, 0])
    a = np.random.permutation(np.resize(levels, k // 512 * 4)).reshape(k // 512, 4)
    idx = np.arange(k)
    return np.exp2(a[idx // 512, idx % 128 // 32])


BF16 = ml_dtypes.bfloat16


def bf(x):
    return np.asarray(x, np.float32).astype(BF16)


def f64(x):
    return np.asarray(x).astype(np.float64)


NSMP, NA, DOUT, REALNA = 2048, 512, 256, 520


def setup_inputs():
    s = mx_kscale(NA)
    inp = np.random.uniform(0.0, 1.0, (NSMP, REALNA + NSMP))
    g = 0.2 + 1.8 * np.random.uniform(0.0, 1.0, NSMP)
    inp[:, REALNA - 8:REALNA + NSMP - 8] *= g
    inp[:, :NA] = np.random.standard_normal((NSMP, NA)) * s
    return {"input": bf(inp), "weight": bf(np.random.standard_normal((NA, DOUT)) * 6.0 / np.sqrt(NA) / s[:, None])}


def reference(input, weight):
    inp = f64(input)
    nSmp = NSMP
    na = NA
    X = inp[:, :na]
    realna = inp.shape[1] - nSmp
    A = inp[:, realna - 8:realna + nSmp - 8]
    A = A + np.eye(nSmp)
    d = np.sum(A, axis=0)
    d_inv_sqrt = 1.0 / np.sqrt(d)
    DAD = d_inv_sqrt[:, None] * A * d_inv_sqrt[None, :]
    support = mxq(X, 1, "e4m3") @ mxq(f64(weight), 0, "e4m3")
    output = mxq(DAD, 1, "e4m3") @ mxq(support, 0, "e4m3")
    return np.concatenate((output, A), axis=1)

@@ -1,0 +1,348 @@
+from contextlib import ExitStack
+
+import concourse.mybir as mybir
+from concourse.masks import make_identity
+
+F32 = mybir.dt.float32
+BF16 = mybir.dt.bfloat16
+U32 = mybir.dt.uint32
+U8 = mybir.dt.uint8
+FP8X4 = mybir.dt.float8_e4m3fn_x4
+ALU = mybir.AluOpType
+ACT = mybir.ActivationFunctionType
+AX = mybir.AxisListType
+
+P = 128
+NT = 16
+HALF = 1024
+FLOPS = 2 * 2048 * 512 * 256 + 2 * 2048 * 2048 * 256
+
+PIN = True
+
+MULT_ON_G = ()
+CAST_AT = {-1: (8, 9, 10), 2: (11,), 3: (12,), 4: (13,), 5: (14,), 6: (15,), 7: (0,), 8: (1,), 9: (2,), 10: (3,), 11: (4,), 12: (5,), 13: (6,), 14: (7,)}
+D1_AT = {-2: (0, 1, 2, 3)}
+PART2_ORDER = (8, 9, 10, 11, 12, 13, 14, 15, 0, 1, 2, 3, 4, 5, 6, 7)
+
+
+def units_of(c):
+    if c < 4:
+        return ((2 * c, 0), (2 * c + 1, 0))
+    if c < 8:
+        return ((2 * (c - 4), 1), (2 * (c - 4) + 1, 1))
+    return ((c, 0), (c, 1))
+
+
+def tile_crossviewgcn_layer1_kernel(tc, inp, weight, out):
+    nc = tc.nc
+    with ExitStack() as ctx:
+        if PIN:
+            ctx.enter_context(tc.manual_schedule())
+        const = ctx.enter_context(tc.tile_pool(name="const", bufs=1))
+        big = ctx.enter_context(tc.tile_pool(name="big", bufs=1))
+        work = ctx.enter_context(tc.tile_pool(name="work", bufs=2))
+        psum = ctx.enter_context(tc.psum_pool(name="ps", bufs=5))
+
+        ident = const.tile([P, P], F32, name="ident")
+        make_identity(nc, ident[:])
+        ones = const.tile([P, 2], BF16, name="ones")
+        nc.vector.memset(ones[:], 1.0)
+        onecol = const.tile([P, 1], F32, name="onecol")
+        nc.vector.memset(onecol[:], 1.0)
+        warm = const.tile([P, 1], F32, name="warm")
+        nc.scalar.activation(out=warm[:], in_=onecol[:], func=ACT.Sqrt)
+
+        a32 = [big.tile([P, 2 * HALF], F32, name="a32_%d" % k, offset=k * 8192) for k in range(NT)]
+        st1 = [
+            big.tile([P, 512 + HALF], BF16, name="st1_%d" % k, offset=((k + 1) * 8192 + 4096) if k < NT - 1 else NT * 8192)
+            for k in range(NT)
+        ]
+        st2 = [const.tile([P, HALF], BF16, name="st2_%d" % k) for k in range(NT)]
+        wraw = const.tile([P, 4, 256], BF16, name="wraw")
+        wg = const.tile([P, 256, 4], BF16, name="wg", align_bytes=64)
+        wcodes = const.tile([P, 256], U32, name="wcodes", align_bytes=64)
+        wscl = const.tile([P, 256], U8, name="wscl", align_bytes=64)
+        scodes = const.tile([P, 4, 256], U32, name="scodes", align_bytes=64)
+        sscl = const.tile([P, 4, 256], U8, name="sscl", align_bytes=64)
+        small = {}
+        for part in range(2):
+            for nm in ("dsum", "dp1", "sq", "y0", "uu", "vv", "r"):
+                small[(nm, part)] = const.tile([P, 8], F32, name="%s%d" % (nm, part))
+        r = [small[("r", 0)], small[("r", 1)]]
+
+        for u in range(2):
+            nc.sync.dma_start(
+                out=wraw[:, 2 * u : 2 * u + 2, :],
+                in_=weight[256 * u : 256 * u + 256, :].rearrange("(p e) n -> p e n", e=2),
+            )
+        for k in range(NT):
+            nc.sync.dma_start(out=st1[k][:], in_=inp[k * P : (k + 1) * P, 0 : 512 + HALF])
+        for k in PART2_ORDER:
+            nc.sync.dma_start(out=st2[k][:], in_=inp[k * P : (k + 1) * P, 512 + HALF : 512 + 2 * HALF])
+
+        state = {}
+        dps = {}
+        xcodes = {}
+        bt = {}
+        banks = {}
+        grs = {}
+        codes = {}
+        accs = {}
+        toks = {}
+
+        def new_codes(key):
+            cw = work.tile([P, 512], U32, tag="codes", bufs=7, name="cw", align_bytes=64)
+            cs = work.tile([P, 512], U8, tag="scl", bufs=7, name="cs", align_bytes=64)
+            codes[key] = (cw, cs)
+            return cw, cs
+
+        def colsum_mm(k, part):
+            src = st1[k][:, 512 : 512 + HALF] if part == 0 else st2[k]
+            for b in range(8):
+                nc.tensor.matmul(
+                    out=dps[part][:, b * NT + k : b * NT + k + 1],
+                    lhsT=src[:, b * P : (b + 1) * P],
+                    rhs=ones[:, 0:1],
+                    start=True,
+                    stop=True,
+                )
+
+        def x_transposes(k):
+            if k % 2 == 0:
+                state["xt"] = psum.tile([P, 2, 2, P], F32, tag="t", name="xt")
+            xw = st1[k][:].bitcast(F32)
+            for u in range(2):
+                nc.tensor.transpose(out=state["xt"][:, k % 2, u, :], in_=xw[:, u * P : (u + 1) * P], identity=ident[:])
+
+        def x_evac(k):
+            if k % 4 == 1:
+                state["xg"] = work.tile([P, 4, P, 4], BF16, tag="gr", bufs=3, name="xg", align_bytes=64)
+            view = (
+                state["xg"][:]
+                .rearrange("p n i t -> p (n i t)")
+                .bitcast(F32)
+                .rearrange("p (n i u) -> p n i u", n=4, u=2)
+            )
+            n0 = (k - 1) % 4
+            nc.scalar.copy(out=view[:, n0 : n0 + 2, :, :], in_=state["xt"][:].rearrange("p n u i -> p n i u"))
+
+        def x_quant(g):
+            cw, cs = new_codes(("x", g))
+            nc.vector.quantize_mx(
+                out=cw[:].bitcast(FP8X4), scales=cs[:], in_=state["xg"][:].rearrange("p n i t -> p (n i t)")
+            )
+
+        def mx1(g):
+            cw, cs = codes[("x", g)]
+            sp = []
+            for nh in range(2):
+                spt = psum.tile([P, 4, P], F32, tag="t", name="sp")
+                for t in range(4):
+                    nc.tensor.matmul_mx(
+                        out=spt[:, t, :],
+                        lhsT=cw[:, t * P : (t + 1) * P].bitcast(FP8X4),
+                        lhsT_scale=cs[:, t * P : (t + 1) * P],
+                        rhs=wcodes[:, nh * P : (nh + 1) * P].bitcast(FP8X4),
+                        rhs_scale=wscl[:, nh * P : (nh + 1) * P],
+                        start=True,
+                        stop=True,
+                    )
+                sp.append(spt)
+            state[("sp", g)] = sp
+
+        def s_evac(g):
+            sg = work.tile([P, 256, 4], BF16, tag="sg", bufs=2, name="sg", align_bytes=64)
+            for nh in range(2):
+                nc.scalar.copy(
+                    out=sg[:, nh * P : (nh + 1) * P, :], in_=state[("sp", g)][nh][:].rearrange("p t n -> p n t")
+                )
+            state[("sg", g)] = sg
+
+        def s_quant(g):
+            nc.vector.quantize_mx(
+                out=scodes[:, g, :].bitcast(FP8X4),
+                scales=sscl[:, g, :],
+                in_=state[("sg", g)][:].rearrange("p n t -> p (n t)"),
+            )
+
+        def cast0(k):
+            nc.vector.tensor_copy(out=a32[k][:, 0:HALF], in_=st1[k][:, 512 : 512 + HALF])
+            if k < 8:
+                blk = a32[k][:, k * P : (k + 1) * P]
+                nc.vector.tensor_tensor(out=blk, in0=blk, in1=ident[:], op=ALU.add)
+
+        def cast1(k, tk):
+            nc.gpsimd.tensor_scalar(
+                out=a32[k][:, HALF : 2 * HALF],
+                in0=st2[k][:],
+                scalar1=1.0,
+                scalar2=(0.0 if tk is None else tk[:]),
+                op0=ALU.mult,
+                op1=ALU.add,
+            )
+            if k >= 8:
+                blk = a32[k][:, k * P : (k + 1) * P]
+                nc.gpsimd.tensor_tensor(out=blk, in0=blk, in1=ident[:], op=ALU.add)
+            nc.sync.dma_start(out=out[k * P : (k + 1) * P, 256 : 256 + 2 * HALF], in_=a32[k][:])
+
+        def r_reduce(part):
+            nc.vector.tensor_reduce(
+                out=small[("dsum", part)][:],
+                in_=dps[part][:].rearrange("p (b k) -> p b k", k=NT),
+                axis=AX.X,
+                op=ALU.add,
+            )
+            nc.scalar.activation(out=small[("sq", part)][:], in_=small[("dsum", part)][:], func=ACT.Sqrt, bias=onecol[:])
+            nc.vector.tensor_scalar_add(out=small[("dp1", part)][:], in0=small[("dsum", part)][:], scalar1=1.0)
+
+        def r_finish(part):
+            y0 = small[("y0", part)]
+            nc.vector.reciprocal(out=y0[:], in_=small[("sq", part)][:])
+            nc.vector.tensor_tensor(out=small[("uu", part)][:], in0=y0[:], in1=y0[:], op=ALU.mult)
+            nc.vector.scalar_tensor_tensor(
+                out=small[("vv", part)][:],
+                in0=small[("uu", part)][:],
+                scalar=-0.5,
+                in1=small[("dp1", part)][:],
+                op0=ALU.mult,
+                op1=ALU.mult,
+            )
+            nc.vector.scalar_tensor_tensor(
+                out=r[part][:], in0=small[("vv", part)][:], scalar=1.5, in1=y0[:], op0=ALU.add, op1=ALU.mult
+            )
+
+        def mult(c):
+            for ui, (it, h) in enumerate(units_of(c)):
+                b = work.tile([P, HALF], F32, tag="b", bufs=4, name="b")
+                src = st2[it][:] if (h == 1 and it < 8) else a32[it][:, h * HALF : (h + 1) * HALF]
+                rcol = r[it // 8][:, it % 8 : it % 8 + 1]
+                if (c, ui) in MULT_ON_G:
+                    nc.gpsimd.tensor_scalar(out=b[:], in0=src, scalar1=rcol, scalar2=0.0, op0=ALU.mult, op1=ALU.add)
+                else:
+                    nc.scalar.activation(out=b[:], in_=src, func=ACT.Copy, scale=rcol)
+                bt[(c, ui)] = b
+
+        def transposes(c, s):
+            b = bt[(c, s // 2)]
+            gp = s % 2
+            tp = psum.tile([P, 4, P], F32, tag="t", name="tp")
+            for t in range(4):
+                nc.tensor.transpose(
+                    out=tp[:, t, :], in_=b[:, gp * 512 + t * P : gp * 512 + (t + 1) * P], identity=ident[:]
+                )
+            banks[(c, s)] = tp
+
+        def evac(c, s):
+            if s == 0:
+                grs[c] = work.tile([P, 4, P, 4], BF16, tag="gr", bufs=3, name="gr", align_bytes=64)
+            h = units_of(c)[s // 2][1]
+            gp = s % 2
+            nc.vector.tensor_tensor(
+                out=grs[c][:, s, :, :],
+                in0=banks[(c, s)][:].rearrange("p t i -> p i t"),
+                in1=r[h][:, 4 * gp : 4 * gp + 4].unsqueeze(1).to_broadcast([P, P, 4]),
+                op=ALU.mult,
+            )
+
+        def quant(c):
+            cw, cs = new_codes(c)
+            nc.vector.quantize_mx(
+                out=cw[:].bitcast(FP8X4), scales=cs[:], in_=grs[c][:].rearrange("p s i t -> p (s i t)")
+            )
+
+        def token(c):
+            toks[c] = const.tile([P, 1], F32, name="tok%d" % (c + 3))
+            nc.vector.memset(toks[c][:], 0.0)
+
+        def where(it, g):
+            if it < 8:
+                return (it // 2 + (0 if g < 2 else 4), (it % 2) * 2 + g % 2)
+            return (it, g)
+
+        def done_tiles(c):
+            if c < 4:
+                return ()
+            if c < 8:
+                return (2 * (c - 4), 2 * (c - 4) + 1)
+            return (c,)
+
+        def mx2(c):
+            for it in done_tiles(c):
+                acc = psum.tile([P, 256], F32, tag="acc", bufs=2, name="acc")
+                for g in range(4):
+                    cc, s = where(it, g)
+                    cw, cs = codes[cc]
+                    nc.tensor.matmul_mx(
+                        out=acc[:],
+                        lhsT=cw[:, s * P : (s + 1) * P].bitcast(FP8X4),
+                        lhsT_scale=cs[:, s * P : (s + 1) * P],
+                        rhs=scodes[:, g, :].bitcast(FP8X4),
+                        rhs_scale=sscl[:, g, :],
+                        start=(g == 0),
+                        stop=(g == 3),
+                    )
+                accs[it] = acc
+
+        def out_store(c):
+            for it in done_tiles(c):
+                osb = work.tile([P, 256], F32, tag="osb", bufs=4, name="osb")
+                nc.scalar.copy(out=osb[:], in_=accs[it][:])
+                nc.scalar.dma_start(out=out[it * P : (it + 1) * P, 0:256], in_=osb[:])
+
+        nc.vector.tensor_copy(out=wg[:], in_=wraw[:].rearrange("p t n -> p n t"))
+        nc.vector.quantize_mx(out=wcodes[:].bitcast(FP8X4), scales=wscl[:], in_=wg[:].rearrange("p n t -> p (n t)"))
+
+        dall = psum.tile([P, 2, 8 * NT], F32, tag="d", bufs=1, name="dall")
+        dps[0] = dall[:, 0, :]
+        dps[1] = dall[:, 1, :]
+        for k in range(NT):
+            colsum_mm(k, 0)
+            x_transposes(k)
+            cast0(k)
+            if k == NT - 1:
+                r_reduce(0)
+                r_finish(0)
+            if k % 2 == 1:
+                x_evac(k)
+            if k % 4 == 0 and k >= 4:
+                x_quant(k // 4 - 1)
+            if k % 4 == 1 and k >= 5:
+                mx1(k // 4 - 1)
+                s_evac(k // 4 - 1)
+            if k % 4 == 3 and k >= 7:
+                s_quant(k // 4 - 1)
+        x_quant(3)
+        token(-3)
+
+        for c in range(-2, NT + 2):
+            if 0 <= c + 2 < NT:
+                mult(c + 2)
+            for k in CAST_AT.get(c, ()):
+                cast1(k, toks.get(c - 2))
+            if c == 0:
+                s_evac(3)
+            for k in D1_AT.get(c, ()):
+                colsum_mm(PART2_ORDER[k], 1)
+            for s in range(4):
+                if 0 <= c < NT:
+                    evac(c, s)
+                if -1 <= c <= 1:
+                    colsum_mm(PART2_ORDER[4 * (c + 2) + s], 1)
+                if 0 <= c + 1 < NT:
+                    transposes(c + 1, s)
+            if c == -1:
+                mx1(3)
+            if c == 1:
+                s_quant(3)
+            if 0 <= c - 1 < NT:
+                quant(c - 1)
+            if c == 2:
+                r_reduce(1)
+            if c == 3:
+                r_finish(1)
+            if 0 <= c - 1 < NT:
+                token(c - 1)
+            if 0 <= c - 2 < NT:
+                out_store(c - 2)
+            if 0 <= c - 1 < NT:
+                mx2(c - 1)

@@ -18,10 +18,12 @@ HALF = 1024
 FLOPS = 2 * 2048 * 512 * 256 + 2 * 2048 * 2048 * 256
 
 PIN = True
+MX_LAG = 2
+NEWTON = True
 
-MULT_ON_G = ()
-CAST_AT = {-1: (8, 9, 10), 2: (11,), 3: (12,), 4: (13,), 5: (14,), 6: (15,), 7: (0,), 8: (1,), 9: (2,), 10: (3,), 11: (4,), 12: (5,), 13: (6,), 14: (7,)}
-D1_AT = {-2: (0, 1, 2, 3)}
+CAST_AT = {-1: (8, 9, 10), 2: (0,), 3: (1,), 4: (2,), 5: (3,), 6: (11,), 7: (12,), 8: (13,), 9: (14,), 10: (15,), 11: (4,), 12: (5,), 13: (6,), 14: (7,)}
+G_COLS = {4: 512, 5: 512, 6: 512, 7: 512, 13: 512, 14: 512, 15: 512}
+COLSUM_AFTER = {(-1, 3): (5, 6), (0, 1): (7, 8), (0, 3): (9, 10), (1, 1): (11, 12), (1, 3): (13, 14), (2, 0): (15,)}
 PART2_ORDER = (8, 9, 10, 11, 12, 13, 14, 15, 0, 1, 2, 3, 4, 5, 6, 7)
 
 
@@ -41,7 +43,7 @@ def tile_crossviewgcn_layer1_kernel(tc, inp, weight, out):
         const = ctx.enter_context(tc.tile_pool(name="const", bufs=1))
         big = ctx.enter_context(tc.tile_pool(name="big", bufs=1))
         work = ctx.enter_context(tc.tile_pool(name="work", bufs=2))
-        psum = ctx.enter_context(tc.psum_pool(name="ps", bufs=5))
+        psum = ctx.enter_context(tc.psum_pool(name="ps", bufs=6))
 
         ident = const.tile([P, P], F32, name="ident")
         make_identity(nc, ident[:])
@@ -70,19 +72,23 @@ def tile_crossviewgcn_layer1_kernel(tc, inp, weight, out):
                 small[(nm, part)] = const.tile([P, 8], F32, name="%s%d" % (nm, part))
         r = [small[("r", 0)], small[("r", 1)]]
 
+        def load1(k):
+            nc.sync.dma_start(out=st1[k][:], in_=inp[k * P : (k + 1) * P, 0 : 512 + HALF])
+
+        load1(0)
+        load1(1)
         for u in range(2):
             nc.sync.dma_start(
                 out=wraw[:, 2 * u : 2 * u + 2, :],
                 in_=weight[256 * u : 256 * u + 256, :].rearrange("(p e) n -> p e n", e=2),
             )
-        for k in range(NT):
-            nc.sync.dma_start(out=st1[k][:], in_=inp[k * P : (k + 1) * P, 0 : 512 + HALF])
+        for k in range(2, NT):
+            load1(k)
         for k in PART2_ORDER:
             nc.sync.dma_start(out=st2[k][:], in_=inp[k * P : (k + 1) * P, 512 + HALF : 512 + 2 * HALF])
 
         state = {}
         dps = {}
-        xcodes = {}
         bt = {}
         banks = {}
         grs = {}
@@ -91,8 +97,8 @@ def tile_crossviewgcn_layer1_kernel(tc, inp, weight, out):
         toks = {}
 
         def new_codes(key):
-            cw = work.tile([P, 512], U32, tag="codes", bufs=7, name="cw", align_bytes=64)
-            cs = work.tile([P, 512], U8, tag="scl", bufs=7, name="cs", align_bytes=64)
+            cw = work.tile([P, 512], U32, tag="codes", bufs=8, name="cw", align_bytes=64)
+            cs = work.tile([P, 512], U8, tag="scl", bufs=8, name="cs", align_bytes=64)
             codes[key] = (cw, cs)
             return cw, cs
 
@@ -171,15 +177,13 @@ def tile_crossviewgcn_layer1_kernel(tc, inp, weight, out):
                 blk = a32[k][:, k * P : (k + 1) * P]
                 nc.vector.tensor_tensor(out=blk, in0=blk, in1=ident[:], op=ALU.add)
 
-        def cast1(k, tk):
+        def g_scale(dst, src, factor, tk):
             nc.gpsimd.tensor_scalar(
-                out=a32[k][:, HALF : 2 * HALF],
-                in0=st2[k][:],
-                scalar1=1.0,
-                scalar2=(0.0 if tk is None else tk[:]),
-                op0=ALU.mult,
-                op1=ALU.add,
+                out=dst, in0=src, scalar1=factor, scalar2=(0.0 if tk is None else tk[:]), op0=ALU.mult, op1=ALU.add
             )
+
+        def cast1(k, tk):
+            g_scale(a32[k][:, HALF : 2 * HALF], st2[k][:], 1.0, tk)
             if k >= 8:
                 blk = a32[k][:, k * P : (k + 1) * P]
                 nc.gpsimd.tensor_tensor(out=blk, in0=blk, in1=ident[:], op=ALU.add)
@@ -193,9 +197,13 @@ def tile_crossviewgcn_layer1_kernel(tc, inp, weight, out):
                 op=ALU.add,
             )
             nc.scalar.activation(out=small[("sq", part)][:], in_=small[("dsum", part)][:], func=ACT.Sqrt, bias=onecol[:])
-            nc.vector.tensor_scalar_add(out=small[("dp1", part)][:], in0=small[("dsum", part)][:], scalar1=1.0)
+            if NEWTON:
+                nc.vector.tensor_scalar_add(out=small[("dp1", part)][:], in0=small[("dsum", part)][:], scalar1=1.0)
 
         def r_finish(part):
+            if not NEWTON:
+                nc.vector.reciprocal(out=r[part][:], in_=small[("sq", part)][:])
+                return
             y0 = small[("y0", part)]
             nc.vector.reciprocal(out=y0[:], in_=small[("sq", part)][:])
             nc.vector.tensor_tensor(out=small[("uu", part)][:], in0=y0[:], in1=y0[:], op=ALU.mult)
@@ -211,24 +219,46 @@ def tile_crossviewgcn_layer1_kernel(tc, inp, weight, out):
                 out=r[part][:], in0=small[("vv", part)][:], scalar=1.5, in1=y0[:], op0=ALU.add, op1=ALU.mult
             )
 
-        def mult(c):
-            for ui, (it, h) in enumerate(units_of(c)):
-                b = work.tile([P, HALF], F32, tag="b", bufs=4, name="b")
-                src = st2[it][:] if (h == 1 and it < 8) else a32[it][:, h * HALF : (h + 1) * HALF]
-                rcol = r[it // 8][:, it % 8 : it % 8 + 1]
-                if (c, ui) in MULT_ON_G:
-                    nc.gpsimd.tensor_scalar(out=b[:], in0=src, scalar1=rcol, scalar2=0.0, op0=ALU.mult, op1=ALU.add)
-                else:
-                    nc.scalar.activation(out=b[:], in_=src, func=ACT.Copy, scale=rcol)
-                bt[(c, ui)] = b
+        def src_of(it, h, lo, hi):
+            if h == 1 and it < 8:
+                return st2[it][:, lo:hi]
+            return a32[it][:, h * HALF + lo : h * HALF + hi]
+
+        def mult_s(c):
+            b = work.tile([P, 2 * HALF], F32, tag="b", bufs=2, name="b")
+            bt[c] = b
+            gcols = G_COLS.get(c, 0)
+            un = units_of(c)
+            if c >= 8:
+                pieces = [(un[0][0], 0, 0, 2 * HALF - gcols, 0)]
+            elif c == 0:
+                pieces = [(un[0][0], un[0][1], 0, 512, 0), (un[0][0], un[0][1], 512, HALF, 512), (un[1][0], un[1][1], 0, HALF, HALF)]
+            else:
+                pieces = [(un[0][0], un[0][1], 0, HALF, 0), (un[1][0], un[1][1], 0, HALF - gcols, HALF)]
+            for it, h, lo, hi, dst in pieces:
+                nc.scalar.activation(
+                    out=b[:, dst : dst + hi - lo],
+                    in_=src_of(it, h, lo, hi),
+                    func=ACT.Copy,
+                    scale=r[it // 8][:, it % 8 : it % 8 + 1],
+                )
+
+        def mult_g(c, tk):
+            gcols = G_COLS.get(c, 0)
+            if gcols:
+                it, h = units_of(c)[1]
+                g_scale(
+                    bt[c][:, 2 * HALF - gcols : 2 * HALF],
+                    src_of(it, h, HALF - gcols, HALF),
+                    r[it // 8][:, it % 8 : it % 8 + 1],
+                    tk,
+                )
 
         def transposes(c, s):
-            b = bt[(c, s // 2)]
-            gp = s % 2
             tp = psum.tile([P, 4, P], F32, tag="t", name="tp")
             for t in range(4):
                 nc.tensor.transpose(
-                    out=tp[:, t, :], in_=b[:, gp * 512 + t * P : gp * 512 + (t + 1) * P], identity=ident[:]
+                    out=tp[:, t, :], in_=bt[c][:, s * 512 + t * P : s * 512 + (t + 1) * P], identity=ident[:]
                 )
             banks[(c, s)] = tp
 
@@ -244,10 +274,14 @@ def tile_crossviewgcn_layer1_kernel(tc, inp, weight, out):
                 op=ALU.mult,
             )
 
-        def quant(c):
-            cw, cs = new_codes(c)
+        def quant(c, lo=0, hi=4):
+            if lo == 0:
+                new_codes(c)
+            cw, cs = codes[c]
             nc.vector.quantize_mx(
-                out=cw[:].bitcast(FP8X4), scales=cs[:], in_=grs[c][:].rearrange("p s i t -> p (s i t)")
+                out=cw[:, lo * P : hi * P].bitcast(FP8X4),
+                scales=cs[:, lo * P : hi * P],
+                in_=grs[c][:, lo:hi, :, :].rearrange("p s i t -> p (s i t)"),
             )
 
         def token(c):
@@ -260,7 +294,7 @@ def tile_crossviewgcn_layer1_kernel(tc, inp, weight, out):
             return (it, g)
 
         def done_tiles(c):
-            if c < 4:
+            if c < 4 or c >= NT:
                 return ()
             if c < 8:
                 return (2 * (c - 4), 2 * (c - 4) + 1)
@@ -287,18 +321,21 @@ def tile_crossviewgcn_layer1_kernel(tc, inp, weight, out):
             for it in done_tiles(c):
                 osb = work.tile([P, 256], F32, tag="osb", bufs=4, name="osb")
                 nc.scalar.copy(out=osb[:], in_=accs[it][:])
-                nc.scalar.dma_start(out=out[it * P : (it + 1) * P, 0:256], in_=osb[:])
+                nc.sync.dma_start(out=out[it * P : (it + 1) * P, 0:256], in_=osb[:])
 
-        nc.vector.tensor_copy(out=wg[:], in_=wraw[:].rearrange("p t n -> p n t"))
-        nc.vector.quantize_mx(out=wcodes[:].bitcast(FP8X4), scales=wscl[:], in_=wg[:].rearrange("p n t -> p (n t)"))
-
-        dall = psum.tile([P, 2, 8 * NT], F32, tag="d", bufs=1, name="dall")
+        dall = psum.tile([P, 2, 8 * NT], F32, tag="acc", bufs=2, name="dall")
         dps[0] = dall[:, 0, :]
         dps[1] = dall[:, 1, :]
         for k in range(NT):
             colsum_mm(k, 0)
             x_transposes(k)
             cast0(k)
+            if k == 1:
+                nc.vector.tensor_copy(out=wg[:], in_=wraw[:].rearrange("p t n -> p n t"))
+            if k == 2:
+                nc.vector.quantize_mx(
+                    out=wcodes[:].bitcast(FP8X4), scales=wscl[:], in_=wg[:].rearrange("p n t -> p (n t)")
+                )
             if k == NT - 1:
                 r_reduce(0)
                 r_finish(0)
@@ -314,35 +351,43 @@ def tile_crossviewgcn_layer1_kernel(tc, inp, weight, out):
         x_quant(3)
         token(-3)
 
-        for c in range(-2, NT + 2):
+        for c in range(-2, NT + MX_LAG + 2):
+            tk = toks.get(c - 2)
             if 0 <= c + 2 < NT:
-                mult(c + 2)
+                mult_s(c + 2)
             for k in CAST_AT.get(c, ()):
-                cast1(k, toks.get(c - 2))
-            if c == 0:
+                cast1(k, tk)
+                tk = None
+            if 0 <= c + 2 < NT:
+                mult_g(c + 2, tk)
+            if c == 4:
                 s_evac(3)
-            for k in D1_AT.get(c, ()):
-                colsum_mm(PART2_ORDER[k], 1)
+            if c == -2:
+                for k in range(5):
+                    colsum_mm(PART2_ORDER[k], 1)
             for s in range(4):
                 if 0 <= c < NT:
                     evac(c, s)
-                if -1 <= c <= 1:
-                    colsum_mm(PART2_ORDER[4 * (c + 2) + s], 1)
+                if c == NT - 1 and s == 1:
+                    quant(c - 1)
+                    quant(c, 0, 2)
                 if 0 <= c + 1 < NT:
                     transposes(c + 1, s)
-            if c == -1:
+                for k in COLSUM_AFTER.get((c, s), ()):
+                    colsum_mm(PART2_ORDER[k], 1)
+            if c == 3:
                 mx1(3)
-            if c == 1:
+            if c == 5:
                 s_quant(3)
-            if 0 <= c - 1 < NT:
+            if 0 <= c - 1 < NT - 2:
                 quant(c - 1)
+            if c == NT - 1:
+                quant(c, 2, 4)
             if c == 2:
                 r_reduce(1)
             if c == 3:
                 r_finish(1)
-            if 0 <= c - 1 < NT:
+            if 0 <= c - 1 < NT - 2:
                 token(c - 1)
-            if 0 <= c - 2 < NT:
-                out_store(c - 2)
-            if 0 <= c - 1 < NT:
-                mx2(c - 1)
+            out_store(c - MX_LAG - 1)
+            mx2(c - MX_LAG)

@@ -20,10 +20,12 @@ FLOPS = 2 * 2048 * 512 * 256 + 2 * 2048 * 2048 * 256
 PIN = True
 MX_LAG = 2
 NEWTON = True
+ONES_N = (2, 52)
+DBASE = (0, 192)
 
 CAST_AT = {-1: (8, 9, 10), 2: (0,), 3: (1,), 4: (2,), 5: (3,), 6: (11,), 7: (12,), 8: (13,), 9: (14,), 10: (15,), 11: (4,), 12: (5,), 13: (6,), 14: (7,)}
 G_COLS = {4: 512, 5: 512, 6: 512, 7: 512, 13: 512, 14: 512, 15: 512}
-COLSUM_AFTER = {(-1, 3): (5, 6), (0, 1): (7, 8), (0, 3): (9, 10), (1, 1): (11, 12), (1, 3): (13, 14), (2, 0): (15,)}
+COLSUM_AFTER = {(-1, 1): (3,), (-1, 3): (4, 5), (0, 1): (6, 7), (0, 3): (8, 9), (1, 1): (10, 11), (1, 3): (12, 13), (2, 0): (14,), (2, 1): (15,)}
 PART2_ORDER = (8, 9, 10, 11, 12, 13, 14, 15, 0, 1, 2, 3, 4, 5, 6, 7)
 
 
@@ -47,7 +49,7 @@ def tile_crossviewgcn_layer1_kernel(tc, inp, weight, out):
 
         ident = const.tile([P, P], F32, name="ident")
         make_identity(nc, ident[:])
-        ones = const.tile([P, 2], BF16, name="ones")
+        ones = const.tile([P, 64], BF16, name="ones")
         nc.vector.memset(ones[:], 1.0)
         onecol = const.tile([P, 1], F32, name="onecol")
         nc.vector.memset(onecol[:], 1.0)
@@ -87,8 +89,8 @@ def tile_crossviewgcn_layer1_kernel(tc, inp, weight, out):
         for k in PART2_ORDER:
             nc.sync.dma_start(out=st2[k][:], in_=inp[k * P : (k + 1) * P, 512 + HALF : 512 + 2 * HALF])
 
+        dall = psum.tile([P, 512], F32, tag="acc", bufs=2, name="dall")
         state = {}
-        dps = {}
         bt = {}
         banks = {}
         grs = {}
@@ -104,11 +106,14 @@ def tile_crossviewgcn_layer1_kernel(tc, inp, weight, out):
 
         def colsum_mm(k, part):
             src = st1[k][:, 512 : 512 + HALF] if part == 0 else st2[k]
+            n = ONES_N[part]
+            pos = k if part == 0 else PART2_ORDER.index(k)
             for b in range(8):
+                col = DBASE[part] + pos * 8 + b
                 nc.tensor.matmul(
-                    out=dps[part][:, b * NT + k : b * NT + k + 1],
+                    out=dall[:, col : col + n],
                     lhsT=src[:, b * P : (b + 1) * P],
-                    rhs=ones[:, 0:1],
+                    rhs=ones[:, 0:n],
                     start=True,
                     stop=True,
                 )
@@ -192,7 +197,7 @@ def tile_crossviewgcn_layer1_kernel(tc, inp, weight, out):
         def r_reduce(part):
             nc.vector.tensor_reduce(
                 out=small[("dsum", part)][:],
-                in_=dps[part][:].rearrange("p (b k) -> p b k", k=NT),
+                in_=dall[:, DBASE[part] : DBASE[part] + 8 * NT].rearrange("p (k b) -> p b k", b=8),
                 axis=AX.X,
                 op=ALU.add,
             )
@@ -323,9 +328,6 @@ def tile_crossviewgcn_layer1_kernel(tc, inp, weight, out):
                 nc.scalar.copy(out=osb[:], in_=accs[it][:])
                 nc.sync.dma_start(out=out[it * P : (it + 1) * P, 0:256], in_=osb[:])
 
-        dall = psum.tile([P, 2, 8 * NT], F32, tag="acc", bufs=2, name="dall")
-        dps[0] = dall[:, 0, :]
-        dps[1] = dall[:, 1, :]
         for k in range(NT):
             colsum_mm(k, 0)
             x_transposes(k)
@@ -343,10 +345,10 @@ def tile_crossviewgcn_layer1_kernel(tc, inp, weight, out):
                 x_evac(k)
             if k % 4 == 0 and k >= 4:
                 x_quant(k // 4 - 1)
-            if k % 4 == 1 and k >= 5:
+            if k % 4 == 1 and 5 <= k < 13:
                 mx1(k // 4 - 1)
                 s_evac(k // 4 - 1)
-            if k % 4 == 3 and k >= 7:
+            if k % 4 == 3 and 7 <= k < 15:
                 s_quant(k // 4 - 1)
         x_quant(3)
         token(-3)
@@ -360,10 +362,10 @@ def tile_crossviewgcn_layer1_kernel(tc, inp, weight, out):
                 tk = None
             if 0 <= c + 2 < NT:
                 mult_g(c + 2, tk)
-            if c == 4:
-                s_evac(3)
+            if c == 2 or c == 4:
+                s_evac((c + 2) // 2)
             if c == -2:
-                for k in range(5):
+                for k in range(3):
                     colsum_mm(PART2_ORDER[k], 1)
             for s in range(4):
                 if 0 <= c < NT:
@@ -375,10 +377,10 @@ def tile_crossviewgcn_layer1_kernel(tc, inp, weight, out):
                     transposes(c + 1, s)
                 for k in COLSUM_AFTER.get((c, s), ()):
                     colsum_mm(PART2_ORDER[k], 1)
-            if c == 3:
-                mx1(3)
-            if c == 5:
-                s_quant(3)
+            if c == 1 or c == 3:
+                mx1((c + 3) // 2)
+            if c == 3 or c == 5:
+                s_quant((c + 1) // 2)
             if 0 <= c - 1 < NT - 2:
                 quant(c - 1)
             if c == NT - 1:

@@ -20,6 +20,7 @@ FLOPS = 2 * 2048 * 512 * 256 + 2 * 2048 * 2048 * 256
 PIN = True
 MX_LAG = 2
 NEWTON = True
+ARS = True
 ONES_N = (2, 52)
 DBASE = (0, 192)
 
@@ -54,7 +55,7 @@ def tile_crossviewgcn_layer1_kernel(tc, inp, weight, out):
         onecol = const.tile([P, 1], F32, name="onecol")
         nc.vector.memset(onecol[:], 1.0)
         warm = const.tile([P, 1], F32, name="warm")
-        nc.scalar.activation(out=warm[:], in_=onecol[:], func=ACT.Sqrt)
+        nc.scalar.activation(out=warm[:], in_=onecol[:], func=(ACT.Abs_reciprocal_sqrt if ARS else ACT.Sqrt))
 
         a32 = [big.tile([P, 2 * HALF], F32, name="a32_%d" % k, offset=k * 8192) for k in range(NT)]
         st1 = [
@@ -70,7 +71,7 @@ def tile_crossviewgcn_layer1_kernel(tc, inp, weight, out):
         sscl = const.tile([P, 4, 256], U8, name="sscl", align_bytes=64)
         small = {}
         for part in range(2):
-            for nm in ("dsum", "dp1", "sq", "y0", "uu", "vv", "r"):
+            for nm in ("dsum", "r") if ARS else ("dsum", "dp1", "sq", "y0", "uu", "vv", "r"):
                 small[(nm, part)] = const.tile([P, 8], F32, name="%s%d" % (nm, part))
         r = [small[("r", 0)], small[("r", 1)]]
 
@@ -201,11 +202,18 @@ def tile_crossviewgcn_layer1_kernel(tc, inp, weight, out):
                 axis=AX.X,
                 op=ALU.add,
             )
+            if ARS:
+                nc.scalar.activation(
+                    out=r[part][:], in_=small[("dsum", part)][:], func=ACT.Abs_reciprocal_sqrt, bias=onecol[:]
+                )
+                return
             nc.scalar.activation(out=small[("sq", part)][:], in_=small[("dsum", part)][:], func=ACT.Sqrt, bias=onecol[:])
             if NEWTON:
                 nc.vector.tensor_scalar_add(out=small[("dp1", part)][:], in0=small[("dsum", part)][:], scalar1=1.0)
 
         def r_finish(part):
+            if ARS:
+                return
             if not NEWTON:
                 nc.vector.reciprocal(out=r[part][:], in_=small[("sq", part)][:])
                 return

@@ -24,9 +24,12 @@ ARS = True
 ONES_N = (2, 52)
 DBASE = (0, 192)
 
-CAST_AT = {-1: (8, 9, 10), 2: (0,), 3: (1,), 4: (2,), 5: (3,), 6: (11,), 7: (12,), 8: (13,), 9: (14,), 10: (15,), 11: (4,), 12: (5,), 13: (6,), 14: (7,)}
-G_COLS = {4: 512, 5: 512, 6: 512, 7: 512, 13: 512, 14: 512, 15: 512}
+V_CASTS = (8, 9)
+CAST_AT = {-1: (10, 11, 12), 2: (0,), 3: (1,), 4: (2,), 5: (3,), 6: (13,), 7: (14,), 8: (15,), 9: (4,), 10: (5,), 11: (6,), 12: (7,)}
+G_COLS = {4: 512, 5: 512, 6: 512, 7: 512, 11: 512, 12: 512, 13: 512, 14: 512, 15: 1024}
 COLSUM_AFTER = {(-1, 1): (3,), (-1, 3): (4, 5), (0, 1): (6, 7), (0, 3): (8, 9), (1, 1): (10, 11), (1, 3): (12, 13), (2, 0): (14,), (2, 1): (15,)}
+EARLY = {"xq": {6: 0, 10: 1, 14: 2}, "mx1": {7: 0, 11: 1}, "sev": {7: 0, 11: 1}, "sq": {10: 0, 14: 1}}
+STEP = {"xq": {1: 3}, "mx1": {1: 2, 3: 3}, "sev": {2: 2, 4: 3}, "sq": {3: 2, 5: 3}}
 PART2_ORDER = (8, 9, 10, 11, 12, 13, 14, 15, 0, 1, 2, 3, 4, 5, 6, 7)
 
 
@@ -128,9 +131,9 @@ def tile_crossviewgcn_layer1_kernel(tc, inp, weight, out):
 
         def x_evac(k):
             if k % 4 == 1:
-                state["xg"] = work.tile([P, 4, P, 4], BF16, tag="gr", bufs=3, name="xg", align_bytes=64)
+                state[("xg", k // 4)] = work.tile([P, 4, P, 4], BF16, tag="gr", bufs=3, name="xg", align_bytes=64)
             view = (
-                state["xg"][:]
+                state[("xg", k // 4)][:]
                 .rearrange("p n i t -> p (n i t)")
                 .bitcast(F32)
                 .rearrange("p (n i u) -> p n i u", n=4, u=2)
@@ -141,7 +144,7 @@ def tile_crossviewgcn_layer1_kernel(tc, inp, weight, out):
         def x_quant(g):
             cw, cs = new_codes(("x", g))
             nc.vector.quantize_mx(
-                out=cw[:].bitcast(FP8X4), scales=cs[:], in_=state["xg"][:].rearrange("p n i t -> p (n i t)")
+                out=cw[:].bitcast(FP8X4), scales=cs[:], in_=state[("xg", g)][:].rearrange("p n i t -> p (n i t)")
             )
 
         def mx1(g):
@@ -193,6 +196,12 @@ def tile_crossviewgcn_layer1_kernel(tc, inp, weight, out):
             if k >= 8:
                 blk = a32[k][:, k * P : (k + 1) * P]
                 nc.gpsimd.tensor_tensor(out=blk, in0=blk, in1=ident[:], op=ALU.add)
+            nc.sync.dma_start(out=out[k * P : (k + 1) * P, 256 : 256 + 2 * HALF], in_=a32[k][:])
+
+        def cast1_v(k):
+            nc.vector.tensor_copy(out=a32[k][:, HALF : 2 * HALF], in_=st2[k][:])
+            blk = a32[k][:, k * P : (k + 1) * P]
+            nc.vector.tensor_tensor(out=blk, in0=blk, in1=ident[:], op=ALU.add)
             nc.sync.dma_start(out=out[k * P : (k + 1) * P, 256 : 256 + 2 * HALF], in_=a32[k][:])
 
         def r_reduce(part):
@@ -334,32 +343,39 @@ def tile_crossviewgcn_layer1_kernel(tc, inp, weight, out):
             for it in done_tiles(c):
                 osb = work.tile([P, 256], F32, tag="osb", bufs=4, name="osb")
                 nc.scalar.copy(out=osb[:], in_=accs[it][:])
-                nc.sync.dma_start(out=out[it * P : (it + 1) * P, 0:256], in_=osb[:])
+                queue = nc.scalar if it >= NT - 2 else nc.sync
+                queue.dma_start(out=out[it * P : (it + 1) * P, 0:256], in_=osb[:])
+
+        def x_path(table, key):
+            if key in table["xq"]:
+                x_quant(table["xq"][key])
+            if key in table["mx1"]:
+                mx1(table["mx1"][key])
+            if key in table["sev"]:
+                s_evac(table["sev"][key])
+            if key in table["sq"]:
+                s_quant(table["sq"][key])
 
         for k in range(NT):
             colsum_mm(k, 0)
             x_transposes(k)
+            if k == NT - 1:
+                r_reduce(0)
+                r_finish(0)
             cast0(k)
+            if k == NT - 1:
+                for kk in V_CASTS:
+                    cast1_v(kk)
+                token(-3)
             if k == 1:
                 nc.vector.tensor_copy(out=wg[:], in_=wraw[:].rearrange("p t n -> p n t"))
             if k == 2:
                 nc.vector.quantize_mx(
                     out=wcodes[:].bitcast(FP8X4), scales=wscl[:], in_=wg[:].rearrange("p n t -> p (n t)")
                 )
-            if k == NT - 1:
-                r_reduce(0)
-                r_finish(0)
-            if k % 2 == 1:
+            if k % 2 == 1 and k < NT - 1:
                 x_evac(k)
-            if k % 4 == 0 and k >= 4:
-                x_quant(k // 4 - 1)
-            if k % 4 == 1 and 5 <= k < 13:
-                mx1(k // 4 - 1)
-                s_evac(k // 4 - 1)
-            if k % 4 == 3 and 7 <= k < 15:
-                s_quant(k // 4 - 1)
-        x_quant(3)
-        token(-3)
+            x_path(EARLY, k)
 
         for c in range(-2, NT + MX_LAG + 2):
             tk = toks.get(c - 2)
@@ -370,8 +386,10 @@ def tile_crossviewgcn_layer1_kernel(tc, inp, weight, out):
                 tk = None
             if 0 <= c + 2 < NT:
                 mult_g(c + 2, tk)
-            if c == 2 or c == 4:
-                s_evac((c + 2) // 2)
+            if c == -1:
+                x_evac(NT - 1)
+            if c in STEP["sev"]:
+                s_evac(STEP["sev"][c])
             if c == -2:
                 for k in range(3):
                     colsum_mm(PART2_ORDER[k], 1)
@@ -385,10 +403,12 @@ def tile_crossviewgcn_layer1_kernel(tc, inp, weight, out):
                     transposes(c + 1, s)
                 for k in COLSUM_AFTER.get((c, s), ()):
                     colsum_mm(PART2_ORDER[k], 1)
-            if c == 1 or c == 3:
-                mx1((c + 3) // 2)
-            if c == 3 or c == 5:
-                s_quant((c + 1) // 2)
+            if c in STEP["mx1"]:
+                mx1(STEP["mx1"][c])
+            if c in STEP["sq"]:
+                s_quant(STEP["sq"][c])
+            if c in STEP["xq"]:
+                x_quant(STEP["xq"][c])
             if 0 <= c - 1 < NT - 2:
                 quant(c - 1)
             if c == NT - 1:

@@ -24,9 +24,10 @@ ARS = True
 ONES_N = (2, 52)
 DBASE = (0, 192)
 
-V_CASTS = (8, 9)
-CAST_AT = {-1: (10, 11, 12), 2: (0,), 3: (1,), 4: (2,), 5: (3,), 6: (13,), 7: (14,), 8: (15,), 9: (4,), 10: (5,), 11: (6,), 12: (7,)}
-G_COLS = {4: 512, 5: 512, 6: 512, 7: 512, 11: 512, 12: 512, 13: 512, 14: 512, 15: 1024}
+X_LATE = 12
+V_CASTS = (8,)
+CAST_AT = {-1: (9, 10), 2: (0,), 3: (1,), 4: (2,), 5: (3,), 6: (11,), 7: (12,), 8: (13,), 9: (14,), 10: (15,), 11: (4,), 12: (5,), 13: (6,), 14: (7,)}
+G_COLS = {}
 COLSUM_AFTER = {(-1, 1): (3,), (-1, 3): (4, 5), (0, 1): (6, 7), (0, 3): (8, 9), (1, 1): (10, 11), (1, 3): (12, 13), (2, 0): (14,), (2, 1): (15,)}
 EARLY = {"xq": {6: 0, 10: 1, 14: 2}, "mx1": {7: 0, 11: 1}, "sev": {7: 0, 11: 1}, "sq": {10: 0, 14: 1}}
 STEP = {"xq": {1: 3}, "mx1": {1: 2, 3: 3}, "sev": {2: 2, 4: 3}, "sq": {3: 2, 5: 3}}
@@ -78,8 +79,14 @@ def tile_crossviewgcn_layer1_kernel(tc, inp, weight, out):
                 small[(nm, part)] = const.tile([P, 8], F32, name="%s%d" % (nm, part))
         r = [small[("r", 0)], small[("r", 1)]]
 
+        xlate = {}
+        late_pairs = []
+
         def load1(k):
-            nc.sync.dma_start(out=st1[k][:], in_=inp[k * P : (k + 1) * P, 0 : 512 + HALF])
+            if k < X_LATE:
+                nc.sync.dma_start(out=st1[k][:], in_=inp[k * P : (k + 1) * P, 0 : 512 + HALF])
+            else:
+                nc.sync.dma_start(out=st1[k][:, 512 : 512 + HALF], in_=inp[k * P : (k + 1) * P, 512 : 512 + HALF])
 
         load1(0)
         load1(1)
@@ -90,6 +97,9 @@ def tile_crossviewgcn_layer1_kernel(tc, inp, weight, out):
             )
         for k in range(2, NT):
             load1(k)
+        for k in range(X_LATE, NT):
+            xlate[k] = const.tile([P, 512], BF16, name="xl%d" % k)
+            nc.sync.dma_start(out=xlate[k][:], in_=inp[k * P : (k + 1) * P, 0:512])
         for k in PART2_ORDER:
             nc.sync.dma_start(out=st2[k][:], in_=inp[k * P : (k + 1) * P, 512 + HALF : 512 + 2 * HALF])
 
@@ -125,7 +135,7 @@ def tile_crossviewgcn_layer1_kernel(tc, inp, weight, out):
         def x_transposes(k):
             if k % 2 == 0:
                 state["xt"] = psum.tile([P, 2, 2, P], F32, tag="t", name="xt")
-            xw = st1[k][:].bitcast(F32)
+            xw = (st1[k] if k < X_LATE else xlate[k])[:].bitcast(F32)
             for u in range(2):
                 nc.tensor.transpose(out=state["xt"][:, k % 2, u, :], in_=xw[:, u * P : (u + 1) * P], identity=ident[:])
 
@@ -343,8 +353,7 @@ def tile_crossviewgcn_layer1_kernel(tc, inp, weight, out):
             for it in done_tiles(c):
                 osb = work.tile([P, 256], F32, tag="osb", bufs=4, name="osb")
                 nc.scalar.copy(out=osb[:], in_=accs[it][:])
-                queue = nc.scalar if it >= NT - 2 else nc.sync
-                queue.dma_start(out=out[it * P : (it + 1) * P, 0:256], in_=osb[:])
+                nc.sync.dma_start(out=out[it * P : (it + 1) * P, 0:256], in_=osb[:])
 
         def x_path(table, key):
             if key in table["xq"]:
@@ -358,7 +367,8 @@ def tile_crossviewgcn_layer1_kernel(tc, inp, weight, out):
 
         for k in range(NT):
             colsum_mm(k, 0)
-            x_transposes(k)
+            if k < X_LATE:
+                x_transposes(k)
             if k == NT - 1:
                 r_reduce(0)
                 r_finish(0)
@@ -373,7 +383,7 @@ def tile_crossviewgcn_layer1_kernel(tc, inp, weight, out):
                 nc.vector.quantize_mx(
                     out=wcodes[:].bitcast(FP8X4), scales=wscl[:], in_=wg[:].rearrange("p n t -> p (n t)")
                 )
-            if k % 2 == 1 and k < NT - 1:
+            if k % 2 == 1 and k < X_LATE:
                 x_evac(k)
             x_path(EARLY, k)
 
@@ -386,10 +396,17 @@ def tile_crossviewgcn_layer1_kernel(tc, inp, weight, out):
                 tk = None
             if 0 <= c + 2 < NT:
                 mult_g(c + 2, tk)
-            if c == -1:
-                x_evac(NT - 1)
             if c in STEP["sev"]:
                 s_evac(STEP["sev"][c])
+            if c == -2:
+                for k in range(X_LATE, NT):
+                    x_transposes(k)
+                    if k % 2 == 1:
+                        late_pairs.append((k, state["xt"]))
+            if c == -1:
+                for k, xt in late_pairs:
+                    state["xt"] = xt
+                    x_evac(k)
             if c == -2:
                 for k in range(3):
                     colsum_mm(PART2_ORDER[k], 1)

@@ -24,10 +24,10 @@ ARS = True
 ONES_N = (2, 52)
 DBASE = (0, 192)
 
-X_LATE = 12
-V_CASTS = (8,)
-CAST_AT = {-1: (9, 10), 2: (0,), 3: (1,), 4: (2,), 5: (3,), 6: (11,), 7: (12,), 8: (13,), 9: (14,), 10: (15,), 11: (4,), 12: (5,), 13: (6,), 14: (7,)}
-G_COLS = {}
+X_LATE = 16
+V_CASTS = ()
+CAST_AT = {-1: (8, 9, 10), 2: (0,), 3: (1,), 4: (2,), 5: (3,), 6: (11,), 7: (12,), 8: (13,), 9: (14,), 10: (15,), 11: (4,), 12: (5,), 13: (6,), 14: (7,)}
+G_COLS = {4: 512, 5: 512, 6: 512, 7: 512, 13: 512, 14: 512, 15: 512}
 COLSUM_AFTER = {(-1, 1): (3,), (-1, 3): (4, 5), (0, 1): (6, 7), (0, 3): (8, 9), (1, 1): (10, 11), (1, 3): (12, 13), (2, 0): (14,), (2, 1): (15,)}
 EARLY = {"xq": {6: 0, 10: 1, 14: 2}, "mx1": {7: 0, 11: 1}, "sev": {7: 0, 11: 1}, "sq": {10: 0, 14: 1}}
 STEP = {"xq": {1: 3}, "mx1": {1: 2, 3: 3}, "sev": {2: 2, 4: 3}, "sq": {3: 2, 5: 3}}
@@ -383,8 +383,10 @@ def tile_crossviewgcn_layer1_kernel(tc, inp, weight, out):
                 nc.vector.quantize_mx(
                     out=wcodes[:].bitcast(FP8X4), scales=wscl[:], in_=wg[:].rearrange("p n t -> p (n t)")
                 )
-            if k % 2 == 1 and k < X_LATE:
+            if k % 2 == 1 and k < min(X_LATE, NT - 1):
                 x_evac(k)
+            if k == NT - 1 and k < X_LATE:
+                late_pairs.append((k, state["xt"]))
             x_path(EARLY, k)
 
         for c in range(-2, NT + MX_LAG + 2):

from contextlib import ExitStack

import concourse.mybir as mybir
from concourse.masks import make_identity

F32 = mybir.dt.float32
BF16 = mybir.dt.bfloat16
U32 = mybir.dt.uint32
U8 = mybir.dt.uint8
FP8X4 = mybir.dt.float8_e4m3fn_x4
ALU = mybir.AluOpType
ACT = mybir.ActivationFunctionType
AX = mybir.AxisListType

P = 128
NT = 16
HALF = 1024
FLOPS = 2 * 2048 * 512 * 256 + 2 * 2048 * 2048 * 256

PIN = True
MX_LAG = 2
NEWTON = True
ARS = True
ONES_N = (2, 52)
DBASE = (0, 192)

X_LATE = 16
V_CASTS = ()
CAST_AT = {-1: (8, 9, 10), 2: (0,), 3: (1,), 4: (2,), 5: (3,), 6: (11,), 7: (12,), 8: (13,), 9: (14,), 10: (15,), 11: (4,), 12: (5,), 13: (6,), 14: (7,)}
G_COLS = {4: 512, 5: 512, 6: 512, 7: 512, 13: 512, 14: 512, 15: 512}
COLSUM_AFTER = {(-1, 1): (3,), (-1, 3): (4, 5), (0, 1): (6, 7), (0, 3): (8, 9), (1, 1): (10, 11), (1, 3): (12, 13), (2, 0): (14,), (2, 1): (15,)}
EARLY = {"xq": {6: 0, 10: 1, 14: 2}, "mx1": {7: 0, 11: 1}, "sev": {7: 0, 11: 1}, "sq": {10: 0, 14: 1}}
STEP = {"xq": {1: 3}, "mx1": {1: 2, 3: 3}, "sev": {2: 2, 4: 3}, "sq": {3: 2, 5: 3}}
PART2_ORDER = (8, 9, 10, 11, 12, 13, 14, 15, 0, 1, 2, 3, 4, 5, 6, 7)


def units_of(c):
    if c < 4:
        return ((2 * c, 0), (2 * c + 1, 0))
    if c < 8:
        return ((2 * (c - 4), 1), (2 * (c - 4) + 1, 1))
    return ((c, 0), (c, 1))


def tile_crossviewgcn_layer1_kernel(tc, inp, weight, out):
    nc = tc.nc
    with ExitStack() as ctx:
        if PIN:
            ctx.enter_context(tc.manual_schedule())
        const = ctx.enter_context(tc.tile_pool(name="const", bufs=1))
        big = ctx.enter_context(tc.tile_pool(name="big", bufs=1))
        work = ctx.enter_context(tc.tile_pool(name="work", bufs=2))
        psum = ctx.enter_context(tc.psum_pool(name="ps", bufs=6))

        ident = const.tile([P, P], F32, name="ident")
        make_identity(nc, ident[:])
        ones = const.tile([P, 64], BF16, name="ones")
        nc.vector.memset(ones[:], 1.0)
        onecol = const.tile([P, 1], F32, name="onecol")
        nc.vector.memset(onecol[:], 1.0)
        warm = const.tile([P, 1], F32, name="warm")
        nc.scalar.activation(out=warm[:], in_=onecol[:], func=(ACT.Abs_reciprocal_sqrt if ARS else ACT.Sqrt))

        a32 = [big.tile([P, 2 * HALF], F32, name="a32_%d" % k, offset=k * 8192) for k in range(NT)]
        st1 = [
            big.tile([P, 512 + HALF], BF16, name="st1_%d" % k, offset=((k + 1) * 8192 + 4096) if k < NT - 1 else NT * 8192)
            for k in range(NT)
        ]
        st2 = [const.tile([P, HALF], BF16, name="st2_%d" % k) for k in range(NT)]
        wraw = const.tile([P, 4, 256], BF16, name="wraw")
        wg = const.tile([P, 256, 4], BF16, name="wg", align_bytes=64)
        wcodes = const.tile([P, 256], U32, name="wcodes", align_bytes=64)
        wscl = const.tile([P, 256], U8, name="wscl", align_bytes=64)
        scodes = const.tile([P, 4, 256], U32, name="scodes", align_bytes=64)
        sscl = const.tile([P, 4, 256], U8, name="sscl", align_bytes=64)
        small = {}
        for part in range(2):
            for nm in ("dsum", "r") if ARS else ("dsum", "dp1", "sq", "y0", "uu", "vv", "r"):
                small[(nm, part)] = const.tile([P, 8], F32, name="%s%d" % (nm, part))
        r = [small[("r", 0)], small[("r", 1)]]

        xlate = {}
        late_pairs = []

        def load1(k):
            if k < X_LATE:
                nc.sync.dma_start(out=st1[k][:], in_=inp[k * P : (k + 1) * P, 0 : 512 + HALF])
            else:
                nc.sync.dma_start(out=st1[k][:, 512 : 512 + HALF], in_=inp[k * P : (k + 1) * P, 512 : 512 + HALF])

        load1(0)
        load1(1)
        for u in range(2):
            nc.sync.dma_start(
                out=wraw[:, 2 * u : 2 * u + 2, :],
                in_=weight[256 * u : 256 * u + 256, :].rearrange("(p e) n -> p e n", e=2),
            )
        for k in range(2, NT):
            load1(k)
        for k in range(X_LATE, NT):
            xlate[k] = const.tile([P, 512], BF16, name="xl%d" % k)
            nc.sync.dma_start(out=xlate[k][:], in_=inp[k * P : (k + 1) * P, 0:512])
        for k in PART2_ORDER:
            nc.sync.dma_start(out=st2[k][:], in_=inp[k * P : (k + 1) * P, 512 + HALF : 512 + 2 * HALF])

        dall = psum.tile([P, 512], F32, tag="acc", bufs=2, name="dall")
        state = {}
        bt = {}
        banks = {}
        grs = {}
        codes = {}
        accs = {}
        toks = {}

        def new_codes(key):
            cw = work.tile([P, 512], U32, tag="codes", bufs=8, name="cw", align_bytes=64)
            cs = work.tile([P, 512], U8, tag="scl", bufs=8, name="cs", align_bytes=64)
            codes[key] = (cw, cs)
            return cw, cs

        def colsum_mm(k, part):
            src = st1[k][:, 512 : 512 + HALF] if part == 0 else st2[k]
            n = ONES_N[part]
            pos = k if part == 0 else PART2_ORDER.index(k)
            for b in range(8):
                col = DBASE[part] + pos * 8 + b
                nc.tensor.matmul(
                    out=dall[:, col : col + n],
                    lhsT=src[:, b * P : (b + 1) * P],
                    rhs=ones[:, 0:n],
                    start=True,
                    stop=True,
                )

        def x_transposes(k):
            if k % 2 == 0:
                state["xt"] = psum.tile([P, 2, 2, P], F32, tag="t", name="xt")
            xw = (st1[k] if k < X_LATE else xlate[k])[:].bitcast(F32)
            for u in range(2):
                nc.tensor.transpose(out=state["xt"][:, k % 2, u, :], in_=xw[:, u * P : (u + 1) * P], identity=ident[:])

        def x_evac(k):
            if k % 4 == 1:
                state[("xg", k // 4)] = work.tile([P, 4, P, 4], BF16, tag="gr", bufs=3, name="xg", align_bytes=64)
            view = (
                state[("xg", k // 4)][:]
                .rearrange("p n i t -> p (n i t)")
                .bitcast(F32)
                .rearrange("p (n i u) -> p n i u", n=4, u=2)
            )
            n0 = (k - 1) % 4
            nc.scalar.copy(out=view[:, n0 : n0 + 2, :, :], in_=state["xt"][:].rearrange("p n u i -> p n i u"))

        def x_quant(g):
            cw, cs = new_codes(("x", g))
            nc.vector.quantize_mx(
                out=cw[:].bitcast(FP8X4), scales=cs[:], in_=state[("xg", g)][:].rearrange("p n i t -> p (n i t)")
            )

        def mx1(g):
            cw, cs = codes[("x", g)]
            sp = []
            for nh in range(2):
                spt = psum.tile([P, 4, P], F32, tag="t", name="sp")
                for t in range(4):
                    nc.tensor.matmul_mx(
                        out=spt[:, t, :],
                        lhsT=cw[:, t * P : (t + 1) * P].bitcast(FP8X4),
                        lhsT_scale=cs[:, t * P : (t + 1) * P],
                        rhs=wcodes[:, nh * P : (nh + 1) * P].bitcast(FP8X4),
                        rhs_scale=wscl[:, nh * P : (nh + 1) * P],
                        start=True,
                        stop=True,
                    )
                sp.append(spt)
            state[("sp", g)] = sp

        def s_evac(g):
            sg = work.tile([P, 256, 4], BF16, tag="sg", bufs=2, name="sg", align_bytes=64)
            for nh in range(2):
                nc.scalar.copy(
                    out=sg[:, nh * P : (nh + 1) * P, :], in_=state[("sp", g)][nh][:].rearrange("p t n -> p n t")
                )
            state[("sg", g)] = sg

        def s_quant(g):
            nc.vector.quantize_mx(
                out=scodes[:, g, :].bitcast(FP8X4),
                scales=sscl[:, g, :],
                in_=state[("sg", g)][:].rearrange("p n t -> p (n t)"),
            )

        def cast0(k):
            nc.vector.tensor_copy(out=a32[k][:, 0:HALF], in_=st1[k][:, 512 : 512 + HALF])
            if k < 8:
                blk = a32[k][:, k * P : (k + 1) * P]
                nc.vector.tensor_tensor(out=blk, in0=blk, in1=ident[:], op=ALU.add)

        def g_scale(dst, src, factor, tk):
            nc.gpsimd.tensor_scalar(
                out=dst, in0=src, scalar1=factor, scalar2=(0.0 if tk is None else tk[:]), op0=ALU.mult, op1=ALU.add
            )

        def cast1(k, tk):
            g_scale(a32[k][:, HALF : 2 * HALF], st2[k][:], 1.0, tk)
            if k >= 8:
                blk = a32[k][:, k * P : (k + 1) * P]
                nc.gpsimd.tensor_tensor(out=blk, in0=blk, in1=ident[:], op=ALU.add)
            nc.sync.dma_start(out=out[k * P : (k + 1) * P, 256 : 256 + 2 * HALF], in_=a32[k][:])

        def cast1_v(k):
            nc.vector.tensor_copy(out=a32[k][:, HALF : 2 * HALF], in_=st2[k][:])
            blk = a32[k][:, k * P : (k + 1) * P]
            nc.vector.tensor_tensor(out=blk, in0=blk, in1=ident[:], op=ALU.add)
            nc.sync.dma_start(out=out[k * P : (k + 1) * P, 256 : 256 + 2 * HALF], in_=a32[k][:])

        def r_reduce(part):
            nc.vector.tensor_reduce(
                out=small[("dsum", part)][:],
                in_=dall[:, DBASE[part] : DBASE[part] + 8 * NT].rearrange("p (k b) -> p b k", b=8),
                axis=AX.X,
                op=ALU.add,
            )
            if ARS:
                nc.scalar.activation(
                    out=r[part][:], in_=small[("dsum", part)][:], func=ACT.Abs_reciprocal_sqrt, bias=onecol[:]
                )
                return
            nc.scalar.activation(out=small[("sq", part)][:], in_=small[("dsum", part)][:], func=ACT.Sqrt, bias=onecol[:])
            if NEWTON:
                nc.vector.tensor_scalar_add(out=small[("dp1", part)][:], in0=small[("dsum", part)][:], scalar1=1.0)

        def r_finish(part):
            if ARS:
                return
            if not NEWTON:
                nc.vector.reciprocal(out=r[part][:], in_=small[("sq", part)][:])
                return
            y0 = small[("y0", part)]
            nc.vector.reciprocal(out=y0[:], in_=small[("sq", part)][:])
            nc.vector.tensor_tensor(out=small[("uu", part)][:], in0=y0[:], in1=y0[:], op=ALU.mult)
            nc.vector.scalar_tensor_tensor(
                out=small[("vv", part)][:],
                in0=small[("uu", part)][:],
                scalar=-0.5,
                in1=small[("dp1", part)][:],
                op0=ALU.mult,
                op1=ALU.mult,
            )
            nc.vector.scalar_tensor_tensor(
                out=r[part][:], in0=small[("vv", part)][:], scalar=1.5, in1=y0[:], op0=ALU.add, op1=ALU.mult
            )

        def src_of(it, h, lo, hi):
            if h == 1 and it < 8:
                return st2[it][:, lo:hi]
            return a32[it][:, h * HALF + lo : h * HALF + hi]

        def mult_s(c):
            b = work.tile([P, 2 * HALF], F32, tag="b", bufs=2, name="b")
            bt[c] = b
            gcols = G_COLS.get(c, 0)
            un = units_of(c)
            if c >= 8:
                pieces = [(un[0][0], 0, 0, 2 * HALF - gcols, 0)]
            elif c == 0:
                pieces = [(un[0][0], un[0][1], 0, 512, 0), (un[0][0], un[0][1], 512, HALF, 512), (un[1][0], un[1][1], 0, HALF, HALF)]
            else:
                pieces = [(un[0][0], un[0][1], 0, HALF, 0), (un[1][0], un[1][1], 0, HALF - gcols, HALF)]
            for it, h, lo, hi, dst in pieces:
                nc.scalar.activation(
                    out=b[:, dst : dst + hi - lo],
                    in_=src_of(it, h, lo, hi),
                    func=ACT.Copy,
                    scale=r[it // 8][:, it % 8 : it % 8 + 1],
                )

        def mult_g(c, tk):
            gcols = G_COLS.get(c, 0)
            if gcols:
                it, h = units_of(c)[1]
                g_scale(
                    bt[c][:, 2 * HALF - gcols : 2 * HALF],
                    src_of(it, h, HALF - gcols, HALF),
                    r[it // 8][:, it % 8 : it % 8 + 1],
                    tk,
                )

        def transposes(c, s):
            tp = psum.tile([P, 4, P], F32, tag="t", name="tp")
            for t in range(4):
                nc.tensor.transpose(
                    out=tp[:, t, :], in_=bt[c][:, s * 512 + t * P : s * 512 + (t + 1) * P], identity=ident[:]
                )
            banks[(c, s)] = tp

        def evac(c, s):
            if s == 0:
                grs[c] = work.tile([P, 4, P, 4], BF16, tag="gr", bufs=3, name="gr", align_bytes=64)
            h = units_of(c)[s // 2][1]
            gp = s % 2
            nc.vector.tensor_tensor(
                out=grs[c][:, s, :, :],
                in0=banks[(c, s)][:].rearrange("p t i -> p i t"),
                in1=r[h][:, 4 * gp : 4 * gp + 4].unsqueeze(1).to_broadcast([P, P, 4]),
                op=ALU.mult,
            )

        def quant(c, lo=0, hi=4):
            if lo == 0:
                new_codes(c)
            cw, cs = codes[c]
            nc.vector.quantize_mx(
                out=cw[:, lo * P : hi * P].bitcast(FP8X4),
                scales=cs[:, lo * P : hi * P],
                in_=grs[c][:, lo:hi, :, :].rearrange("p s i t -> p (s i t)"),
            )

        def token(c):
            toks[c] = const.tile([P, 1], F32, name="tok%d" % (c + 3))
            nc.vector.memset(toks[c][:], 0.0)

        def where(it, g):
            if it < 8:
                return (it // 2 + (0 if g < 2 else 4), (it % 2) * 2 + g % 2)
            return (it, g)

        def done_tiles(c):
            if c < 4 or c >= NT:
                return ()
            if c < 8:
                return (2 * (c - 4), 2 * (c - 4) + 1)
            return (c,)

        def mx2(c):
            for it in done_tiles(c):
                acc = psum.tile([P, 256], F32, tag="acc", bufs=2, name="acc")
                for g in range(4):
                    cc, s = where(it, g)
                    cw, cs = codes[cc]
                    nc.tensor.matmul_mx(
                        out=acc[:],
                        lhsT=cw[:, s * P : (s + 1) * P].bitcast(FP8X4),
                        lhsT_scale=cs[:, s * P : (s + 1) * P],
                        rhs=scodes[:, g, :].bitcast(FP8X4),
                        rhs_scale=sscl[:, g, :],
                        start=(g == 0),
                        stop=(g == 3),
                    )
                accs[it] = acc

        def out_store(c):
            for it in done_tiles(c):
                osb = work.tile([P, 256], F32, tag="osb", bufs=4, name="osb")
                nc.scalar.copy(out=osb[:], in_=accs[it][:])
                nc.sync.dma_start(out=out[it * P : (it + 1) * P, 0:256], in_=osb[:])

        def x_path(table, key):
            if key in table["xq"]:
                x_quant(table["xq"][key])
            if key in table["mx1"]:
                mx1(table["mx1"][key])
            if key in table["sev"]:
                s_evac(table["sev"][key])
            if key in table["sq"]:
                s_quant(table["sq"][key])

        for k in range(NT):
            colsum_mm(k, 0)
            if k < X_LATE:
                x_transposes(k)
            if k == NT - 1:
                r_reduce(0)
                r_finish(0)
            cast0(k)
            if k == NT - 1:
                for kk in V_CASTS:
                    cast1_v(kk)
                token(-3)
            if k == 1:
                nc.vector.tensor_copy(out=wg[:], in_=wraw[:].rearrange("p t n -> p n t"))
            if k == 2:
                nc.vector.quantize_mx(
                    out=wcodes[:].bitcast(FP8X4), scales=wscl[:], in_=wg[:].rearrange("p n t -> p (n t)")
                )
            if k % 2 == 1 and k < min(X_LATE, NT - 1):
                x_evac(k)
            if k == NT - 1 and k < X_LATE:
                late_pairs.append((k, state["xt"]))
            x_path(EARLY, k)

        for c in range(-2, NT + MX_LAG + 2):
            tk = toks.get(c - 2)
            if 0 <= c + 2 < NT:
                mult_s(c + 2)
            for k in CAST_AT.get(c, ()):
                cast1(k, tk)
                tk = None
            if 0 <= c + 2 < NT:
                mult_g(c + 2, tk)
            if c in STEP["sev"]:
                s_evac(STEP["sev"][c])
            if c == -2:
                for k in range(X_LATE, NT):
                    x_transposes(k)
                    if k % 2 == 1:
                        late_pairs.append((k, state["xt"]))
            if c == -1:
                for k, xt in late_pairs:
                    state["xt"] = xt
                    x_evac(k)
            if c == -2:
                for k in range(3):
                    colsum_mm(PART2_ORDER[k], 1)
            for s in range(4):
                if 0 <= c < NT:
                    evac(c, s)
                if c == NT - 1 and s == 1:
                    quant(c - 1)
                    quant(c, 0, 2)
                if 0 <= c + 1 < NT:
                    transposes(c + 1, s)
                for k in COLSUM_AFTER.get((c, s), ()):
                    colsum_mm(PART2_ORDER[k], 1)
            if c in STEP["mx1"]:
                mx1(STEP["mx1"][c])
            if c in STEP["sq"]:
                s_quant(STEP["sq"][c])
            if c in STEP["xq"]:
                x_quant(STEP["xq"][c])
            if 0 <= c - 1 < NT - 2:
                quant(c - 1)
            if c == NT - 1:
                quant(c, 2, 4)
            if c == 2:
                r_reduce(1)
            if c == 3:
                r_finish(1)
            if 0 <= c - 1 < NT - 2:
                token(c - 1)
            out_store(c - MX_LAG - 1)
            mx2(c - MX_LAG)
